import numpy as np
import ml_dtypes

BF16 = ml_dtypes.bfloat16


def bf(x):
    return np.asarray(x, np.float32).astype(BF16)


def f32(x):
    return np.asarray(x, np.float32)


def f64(x):
    return np.asarray(x).astype(np.float64)


def striped(idx):
    return np.tile(idx.reshape(-1, 16).T, (8, 1))


S, D, M, T, V, P, N = 2048, 128, 128, 2, 3, 128, 768
SLOPE = 0.01


def lrelu(a):
    return np.maximum(a, SLOPE * a)


def setup_inputs():
    return {"table": bf(np.random.uniform(0.0, 1.0, (D, S))), "wn": bf(2.0 * np.random.standard_normal((D, M)) / np.sqrt(D)), "bn": f32(0.2 * np.random.standard_normal((M, 1))), "offs": striped(np.random.permutation(S)[:N])}


def reference(table, wn, bn, offs):
    idx = offs[:16].T.reshape(-1)
    h = lrelu(f64(wn).T @ f64(table)[:, idx] + f64(bn))
    return h.reshape(M, T, V, P).sum(axis=2).reshape(M, T * P)

@@ -1,0 +1,51 @@
+import concourse.mybir as mybir
+
+BF16, F32, U16 = mybir.dt.bfloat16, mybir.dt.float32, mybir.dt.uint16
+ALU = mybir.AluOpType
+IDENTITY = mybir.ActivationFunctionType.Identity
+
+STORED = 2048
+FEATURES = 128
+ENCODED = 128
+STEPS, VEHICLES, NODES = 2, 3, 128
+PICKED = STEPS * VEHICLES * NODES
+PIECE = VEHICLES * NODES
+PIECE_COLUMNS = PIECE // 16
+SLOPE = 0.01
+
+FLOPS = 2 * FEATURES * ENCODED * PICKED
+
+
+def tile_gnnbase_kernel(tc, table, wn, bn, offs, out):
+    nc = tc.nc
+    with (
+        tc.tile_pool(name="held", bufs=1) as held,
+        tc.tile_pool(name="work", bufs=2) as work,
+        tc.psum_pool(name="psum", bufs=2) as psum,
+    ):
+        offsets = held.tile([128, PICKED // 16], U16, name="offsets")
+        nc.sync.dma_start(offsets[:], offs)
+        store = held.tile([FEATURES, STORED], BF16, name="store")
+        nc.sync.dma_start(store[:], table)
+        weights = held.tile([FEATURES, ENCODED], BF16, name="weights")
+        nc.scalar.dma_start(weights[:], wn)
+        bias = held.tile([ENCODED, 1], F32, name="bias")
+        nc.scalar.dma_start(bias[:], bn)
+
+        summed = held.tile([ENCODED, STEPS * NODES], F32, name="summed")
+        for t in range(STEPS):
+            projected = psum.tile([ENCODED, PIECE], F32, name="projected")
+            piece = offsets[:, t * PIECE_COLUMNS : (t + 1) * PIECE_COLUMNS]
+            nc.tensor.matmul(projected[:], weights[:], store[:].indirect(piece), start=True, stop=True)
+
+            biased = work.tile([ENCODED, PIECE], F32, name="biased")
+            nc.scalar.activation(biased[:], projected[:], IDENTITY, bias=bias[:])
+
+            encoded = work.tile([ENCODED, PIECE], F32, name="encoded")
+            nc.vector.scalar_tensor_tensor(encoded[:], biased[:], SLOPE, biased[:], ALU.mult, ALU.max)
+
+            pair = work.tile([ENCODED, NODES], F32, name="pair")
+            nc.vector.tensor_add(pair[:], encoded[:, 0:NODES], encoded[:, NODES : 2 * NODES])
+            nc.vector.tensor_add(summed[:, t * NODES : (t + 1) * NODES], pair[:], encoded[:, 2 * NODES : 3 * NODES])
+
+        nc.sync.dma_start(out, summed[:])

@@ -32,6 +32,10 @@ def tile_gnnbase_kernel(tc, table, wn, bn, offs, out):
         bias = held.tile([ENCODED, 1], F32, name="bias")
         nc.scalar.dma_start(bias[:], bn)
 
+        scratch = held.tile([ENCODED, 1], F32, name="scratch")
+        nc.vector.memset(scratch[:], 0.0)
+        nc.scalar.activation(scratch[:], scratch[:], IDENTITY)
+
         summed = held.tile([ENCODED, STEPS * NODES], F32, name="summed")
         for t in range(STEPS):
             projected = psum.tile([ENCODED, PIECE], F32, name="projected")

@@ -9,7 +9,7 @@ FEATURES = 128
 ENCODED = 128
 STEPS, VEHICLES, NODES = 2, 3, 128
 PICKED = STEPS * VEHICLES * NODES
-PIECE = VEHICLES * NODES
+PIECE = NODES
 PIECE_COLUMNS = PIECE // 16
 SLOPE = 0.01
 
@@ -20,8 +20,8 @@ def tile_gnnbase_kernel(tc, table, wn, bn, offs, out):
     nc = tc.nc
     with (
         tc.tile_pool(name="held", bufs=1) as held,
-        tc.tile_pool(name="work", bufs=2) as work,
-        tc.psum_pool(name="psum", bufs=2) as psum,
+        tc.tile_pool(name="work", bufs=3) as work,
+        tc.psum_pool(name="psum", bufs=3) as psum,
     ):
         offsets = held.tile([128, PICKED // 16], U16, name="offsets")
         nc.sync.dma_start(offsets[:], offs)
@@ -38,18 +38,21 @@ def tile_gnnbase_kernel(tc, table, wn, bn, offs, out):
 
         summed = held.tile([ENCODED, STEPS * NODES], F32, name="summed")
         for t in range(STEPS):
-            projected = psum.tile([ENCODED, PIECE], F32, name="projected")
-            piece = offsets[:, t * PIECE_COLUMNS : (t + 1) * PIECE_COLUMNS]
-            nc.tensor.matmul(projected[:], weights[:], store[:].indirect(piece), start=True, stop=True)
+            total = summed[:, t * NODES : (t + 1) * NODES]
+            for v in range(VEHICLES):
+                projected = psum.tile([ENCODED, PIECE], F32, name="projected")
+                first = (t * VEHICLES + v) * PIECE_COLUMNS
+                piece = offsets[:, first : first + PIECE_COLUMNS]
+                nc.tensor.matmul(projected[:], weights[:], store[:].indirect(piece), start=True, stop=True)
 
-            biased = work.tile([ENCODED, PIECE], F32, name="biased")
-            nc.scalar.activation(biased[:], projected[:], IDENTITY, bias=bias[:])
+                biased = work.tile([ENCODED, PIECE], F32, name="biased")
+                nc.scalar.activation(biased[:], projected[:], IDENTITY, bias=bias[:])
 
-            encoded = work.tile([ENCODED, PIECE], F32, name="encoded")
-            nc.vector.scalar_tensor_tensor(encoded[:], biased[:], SLOPE, biased[:], ALU.mult, ALU.max)
-
-            pair = work.tile([ENCODED, NODES], F32, name="pair")
-            nc.vector.tensor_add(pair[:], encoded[:, 0:NODES], encoded[:, NODES : 2 * NODES])
-            nc.vector.tensor_add(summed[:, t * NODES : (t + 1) * NODES], pair[:], encoded[:, 2 * NODES : 3 * NODES])
+                if v == 0:
+                    nc.vector.scalar_tensor_tensor(total, biased[:], SLOPE, biased[:], ALU.mult, ALU.max)
+                else:
+                    encoded = work.tile([ENCODED, PIECE], F32, name="encoded")
+                    nc.vector.scalar_tensor_tensor(encoded[:], biased[:], SLOPE, biased[:], ALU.mult, ALU.max)
+                    nc.vector.tensor_add(total, total, encoded[:])
 
         nc.sync.dma_start(out, summed[:])

@@ -9,9 +9,11 @@ FEATURES = 128
 ENCODED = 128
 STEPS, VEHICLES, NODES = 2, 3, 128
 PICKED = STEPS * VEHICLES * NODES
-PIECE = NODES
+PIECE = VEHICLES * NODES
 PIECE_COLUMNS = PIECE // 16
 SLOPE = 0.01
+WARM_WIDTH = 512
+WARM_MATMULS = 5
 
 FLOPS = 2 * FEATURES * ENCODED * PICKED
 
@@ -20,8 +22,8 @@ def tile_gnnbase_kernel(tc, table, wn, bn, offs, out):
     nc = tc.nc
     with (
         tc.tile_pool(name="held", bufs=1) as held,
-        tc.tile_pool(name="work", bufs=3) as work,
-        tc.psum_pool(name="psum", bufs=3) as psum,
+        tc.tile_pool(name="work", bufs=2) as work,
+        tc.psum_pool(name="psum", bufs=2) as psum,
     ):
         offsets = held.tile([128, PICKED // 16], U16, name="offsets")
         nc.sync.dma_start(offsets[:], offs)
@@ -32,27 +34,30 @@ def tile_gnnbase_kernel(tc, table, wn, bn, offs, out):
         bias = held.tile([ENCODED, 1], F32, name="bias")
         nc.scalar.dma_start(bias[:], bn)
 
+        zeros = held.tile([FEATURES, WARM_WIDTH], BF16, name="zeros")
+        nc.vector.memset(zeros[:], 0.0)
+        unread = psum.tile([ENCODED, WARM_WIDTH], F32, name="unread")
+        for _ in range(WARM_MATMULS):
+            nc.tensor.matmul(unread[:], zeros[:, 0:ENCODED], zeros[:], start=True, stop=True)
+
         scratch = held.tile([ENCODED, 1], F32, name="scratch")
         nc.vector.memset(scratch[:], 0.0)
         nc.scalar.activation(scratch[:], scratch[:], IDENTITY)
 
         summed = held.tile([ENCODED, STEPS * NODES], F32, name="summed")
         for t in range(STEPS):
-            total = summed[:, t * NODES : (t + 1) * NODES]
-            for v in range(VEHICLES):
-                projected = psum.tile([ENCODED, PIECE], F32, name="projected")
-                first = (t * VEHICLES + v) * PIECE_COLUMNS
-                piece = offsets[:, first : first + PIECE_COLUMNS]
-                nc.tensor.matmul(projected[:], weights[:], store[:].indirect(piece), start=True, stop=True)
+            projected = psum.tile([ENCODED, PIECE], F32, name="projected")
+            piece = offsets[:, t * PIECE_COLUMNS : (t + 1) * PIECE_COLUMNS]
+            nc.tensor.matmul(projected[:], weights[:], store[:].indirect(piece), start=True, stop=True)
 
-                biased = work.tile([ENCODED, PIECE], F32, name="biased")
-                nc.scalar.activation(biased[:], projected[:], IDENTITY, bias=bias[:])
+            biased = work.tile([ENCODED, PIECE], F32, name="biased")
+            nc.scalar.activation(biased[:], projected[:], IDENTITY, bias=bias[:])
 
-                if v == 0:
-                    nc.vector.scalar_tensor_tensor(total, biased[:], SLOPE, biased[:], ALU.mult, ALU.max)
-                else:
-                    encoded = work.tile([ENCODED, PIECE], F32, name="encoded")
-                    nc.vector.scalar_tensor_tensor(encoded[:], biased[:], SLOPE, biased[:], ALU.mult, ALU.max)
-                    nc.vector.tensor_add(total, total, encoded[:])
+            encoded = work.tile([ENCODED, PIECE], F32, name="encoded")
+            nc.vector.scalar_tensor_tensor(encoded[:], biased[:], SLOPE, biased[:], ALU.mult, ALU.max)
+
+            pair = work.tile([ENCODED, NODES], F32, name="pair")
+            nc.vector.tensor_add(pair[:], encoded[:, 0:NODES], encoded[:, NODES : 2 * NODES])
+            nc.vector.tensor_add(summed[:, t * NODES : (t + 1) * NODES], pair[:], encoded[:, 2 * NODES : 3 * NODES])
 
         nc.sync.dma_start(out, summed[:])

@@ -12,8 +12,6 @@ PICKED = STEPS * VEHICLES * NODES
 PIECE = VEHICLES * NODES
 PIECE_COLUMNS = PIECE // 16
 SLOPE = 0.01
-WARM_WIDTH = 512
-WARM_MATMULS = 5
 
 FLOPS = 2 * FEATURES * ENCODED * PICKED
 
@@ -34,17 +32,11 @@ def tile_gnnbase_kernel(tc, table, wn, bn, offs, out):
         bias = held.tile([ENCODED, 1], F32, name="bias")
         nc.scalar.dma_start(bias[:], bn)
 
-        zeros = held.tile([FEATURES, WARM_WIDTH], BF16, name="zeros")
-        nc.vector.memset(zeros[:], 0.0)
-        unread = psum.tile([ENCODED, WARM_WIDTH], F32, name="unread")
-        for _ in range(WARM_MATMULS):
-            nc.tensor.matmul(unread[:], zeros[:, 0:ENCODED], zeros[:], start=True, stop=True)
-
         scratch = held.tile([ENCODED, 1], F32, name="scratch")
         nc.vector.memset(scratch[:], 0.0)
         nc.scalar.activation(scratch[:], scratch[:], IDENTITY)
 
-        summed = held.tile([ENCODED, STEPS * NODES], F32, name="summed")
+        encoded = held.tile([ENCODED, PICKED], F32, name="encoded")
         for t in range(STEPS):
             projected = psum.tile([ENCODED, PIECE], F32, name="projected")
             piece = offsets[:, t * PIECE_COLUMNS : (t + 1) * PIECE_COLUMNS]
@@ -53,11 +45,14 @@ def tile_gnnbase_kernel(tc, table, wn, bn, offs, out):
             biased = work.tile([ENCODED, PIECE], F32, name="biased")
             nc.scalar.activation(biased[:], projected[:], IDENTITY, bias=bias[:])
 
-            encoded = work.tile([ENCODED, PIECE], F32, name="encoded")
-            nc.vector.scalar_tensor_tensor(encoded[:], biased[:], SLOPE, biased[:], ALU.mult, ALU.max)
+            nc.vector.scalar_tensor_tensor(
+                encoded[:, t * PIECE : (t + 1) * PIECE], biased[:], SLOPE, biased[:], ALU.mult, ALU.max
+            )
 
-            pair = work.tile([ENCODED, NODES], F32, name="pair")
-            nc.vector.tensor_add(pair[:], encoded[:, 0:NODES], encoded[:, NODES : 2 * NODES])
-            nc.vector.tensor_add(summed[:, t * NODES : (t + 1) * NODES], pair[:], encoded[:, 2 * NODES : 3 * NODES])
+        by_vehicle = encoded[:].rearrange("f (t v n) -> f t v n", t=STEPS, v=VEHICLES)
+        pair = held.tile([ENCODED, STEPS, NODES], F32, name="pair")
+        nc.vector.tensor_add(pair[:], by_vehicle[:, :, 0, :], by_vehicle[:, :, 1, :])
+        summed = held.tile([ENCODED, STEPS, NODES], F32, name="summed")
+        nc.vector.tensor_add(summed[:], pair[:], by_vehicle[:, :, 2, :])
 
-        nc.sync.dma_start(out, summed[:])
+        nc.sync.dma_start(out.rearrange("f (t n) -> f t n", t=STEPS), summed[:])

@@ -23,20 +23,20 @@ def tile_gnnbase_kernel(tc, table, wn, bn, offs, out):
         tc.tile_pool(name="work", bufs=2) as work,
         tc.psum_pool(name="psum", bufs=2) as psum,
     ):
+        store = held.tile([FEATURES, STORED], BF16, name="store")
+        nc.scalar.dma_start(store[:], table)
         offsets = held.tile([128, PICKED // 16], U16, name="offsets")
         nc.sync.dma_start(offsets[:], offs)
-        store = held.tile([FEATURES, STORED], BF16, name="store")
-        nc.sync.dma_start(store[:], table)
         weights = held.tile([FEATURES, ENCODED], BF16, name="weights")
-        nc.scalar.dma_start(weights[:], wn)
+        nc.sync.dma_start(weights[:], wn)
         bias = held.tile([ENCODED, 1], F32, name="bias")
-        nc.scalar.dma_start(bias[:], bn)
+        nc.sync.dma_start(bias[:], bn)
 
         scratch = held.tile([ENCODED, 1], F32, name="scratch")
         nc.vector.memset(scratch[:], 0.0)
         nc.scalar.activation(scratch[:], scratch[:], IDENTITY)
 
-        encoded = held.tile([ENCODED, PICKED], F32, name="encoded")
+        summed = held.tile([ENCODED, STEPS * NODES], F32, name="summed")
         for t in range(STEPS):
             projected = psum.tile([ENCODED, PIECE], F32, name="projected")
             piece = offsets[:, t * PIECE_COLUMNS : (t + 1) * PIECE_COLUMNS]
@@ -45,14 +45,13 @@ def tile_gnnbase_kernel(tc, table, wn, bn, offs, out):
             biased = work.tile([ENCODED, PIECE], F32, name="biased")
             nc.scalar.activation(biased[:], projected[:], IDENTITY, bias=bias[:])
 
-            nc.vector.scalar_tensor_tensor(
-                encoded[:, t * PIECE : (t + 1) * PIECE], biased[:], SLOPE, biased[:], ALU.mult, ALU.max
-            )
+            encoded = work.tile([ENCODED, PIECE], F32, name="encoded")
+            nc.vector.scalar_tensor_tensor(encoded[:], biased[:], SLOPE, biased[:], ALU.mult, ALU.max)
 
-        by_vehicle = encoded[:].rearrange("f (t v n) -> f t v n", t=STEPS, v=VEHICLES)
-        pair = held.tile([ENCODED, STEPS, NODES], F32, name="pair")
-        nc.vector.tensor_add(pair[:], by_vehicle[:, :, 0, :], by_vehicle[:, :, 1, :])
-        summed = held.tile([ENCODED, STEPS, NODES], F32, name="summed")
-        nc.vector.tensor_add(summed[:], pair[:], by_vehicle[:, :, 2, :])
+            pair = work.tile([ENCODED, NODES], F32, name="pair")
+            nc.vector.tensor_add(pair[:], encoded[:, 0:NODES], encoded[:, NODES : 2 * NODES])
+            step = slice(t * NODES, (t + 1) * NODES)
+            nc.vector.tensor_add(summed[:, step], pair[:], encoded[:, 2 * NODES : 3 * NODES])
 
-        nc.sync.dma_start(out.rearrange("f (t n) -> f t n", t=STEPS), summed[:])
+            store_queue = nc.scalar if t == 0 else nc.sync
+            store_queue.dma_start(out[:, step], summed[:, step])

@@ -43,10 +43,13 @@ def tile_gnnbase_kernel(tc, table, wn, bn, offs, out):
             nc.tensor.matmul(projected[:], weights[:], store[:].indirect(piece), start=True, stop=True)
 
             biased = work.tile([ENCODED, PIECE], F32, name="biased")
-            nc.scalar.activation(biased[:], projected[:], IDENTITY, bias=bias[:])
-
             encoded = work.tile([ENCODED, PIECE], F32, name="encoded")
-            nc.vector.scalar_tensor_tensor(encoded[:], biased[:], SLOPE, biased[:], ALU.mult, ALU.max)
+            for v in range(VEHICLES):
+                block = slice(v * NODES, (v + 1) * NODES)
+                nc.scalar.activation(biased[:, block], projected[:, block], IDENTITY, bias=bias[:])
+                nc.vector.scalar_tensor_tensor(
+                    encoded[:, block], biased[:, block], SLOPE, biased[:, block], ALU.mult, ALU.max
+                )
 
             pair = work.tile([ENCODED, NODES], F32, name="pair")
             nc.vector.tensor_add(pair[:], encoded[:, 0:NODES], encoded[:, NODES : 2 * NODES])

@@ -9,8 +9,9 @@ FEATURES = 128
 ENCODED = 128
 STEPS, VEHICLES, NODES = 2, 3, 128
 PICKED = STEPS * VEHICLES * NODES
-PIECE = VEHICLES * NODES
-PIECE_COLUMNS = PIECE // 16
+BLOCKS = STEPS * VEHICLES
+BLOCK_COLUMNS = NODES // 16
+PIECE_BLOCKS = (3, 2, 1)
 SLOPE = 0.01
 
 FLOPS = 2 * FEATURES * ENCODED * PICKED
@@ -21,7 +22,7 @@ def tile_gnnbase_kernel(tc, table, wn, bn, offs, out):
     with (
         tc.tile_pool(name="held", bufs=1) as held,
         tc.tile_pool(name="work", bufs=2) as work,
-        tc.psum_pool(name="psum", bufs=2) as psum,
+        tc.psum_pool(name="psum", bufs=3) as psum,
     ):
         store = held.tile([FEATURES, STORED], BF16, name="store")
         nc.scalar.dma_start(store[:], table)
@@ -36,25 +37,35 @@ def tile_gnnbase_kernel(tc, table, wn, bn, offs, out):
         nc.vector.memset(scratch[:], 0.0)
         nc.scalar.activation(scratch[:], scratch[:], IDENTITY)
 
+        biased = held.tile([ENCODED, PICKED], F32, name="biased")
+        encoded = held.tile([ENCODED, PICKED], F32, name="encoded")
         summed = held.tile([ENCODED, STEPS * NODES], F32, name="summed")
-        for t in range(STEPS):
-            projected = psum.tile([ENCODED, PIECE], F32, name="projected")
-            piece = offsets[:, t * PIECE_COLUMNS : (t + 1) * PIECE_COLUMNS]
-            nc.tensor.matmul(projected[:], weights[:], store[:].indirect(piece), start=True, stop=True)
+        first = 0
+        for blocks in PIECE_BLOCKS:
+            projected = psum.tile([ENCODED, max(PIECE_BLOCKS) * NODES], F32, name="projected")
+            piece = offsets[:, first * BLOCK_COLUMNS : (first + blocks) * BLOCK_COLUMNS]
+            nc.tensor.matmul(
+                projected[:, 0 : blocks * NODES], weights[:], store[:].indirect(piece), start=True, stop=True
+            )
 
-            biased = work.tile([ENCODED, PIECE], F32, name="biased")
-            encoded = work.tile([ENCODED, PIECE], F32, name="encoded")
-            for v in range(VEHICLES):
-                block = slice(v * NODES, (v + 1) * NODES)
-                nc.scalar.activation(biased[:, block], projected[:, block], IDENTITY, bias=bias[:])
+            for b in range(first, first + blocks):
+                block = slice(b * NODES, (b + 1) * NODES)
+                in_piece = slice((b - first) * NODES, (b - first + 1) * NODES)
+                nc.scalar.activation(biased[:, block], projected[:, in_piece], IDENTITY, bias=bias[:])
                 nc.vector.scalar_tensor_tensor(
                     encoded[:, block], biased[:, block], SLOPE, biased[:, block], ALU.mult, ALU.max
                 )
+            first += blocks
 
-            pair = work.tile([ENCODED, NODES], F32, name="pair")
-            nc.vector.tensor_add(pair[:], encoded[:, 0:NODES], encoded[:, NODES : 2 * NODES])
-            step = slice(t * NODES, (t + 1) * NODES)
-            nc.vector.tensor_add(summed[:, step], pair[:], encoded[:, 2 * NODES : 3 * NODES])
-
-            store_queue = nc.scalar if t == 0 else nc.sync
-            store_queue.dma_start(out[:, step], summed[:, step])
+            for b in range(first - blocks, first):
+                t, v = divmod(b, VEHICLES)
+                block = slice(b * NODES, (b + 1) * NODES)
+                before = slice((b - 1) * NODES, b * NODES)
+                step = slice(t * NODES, (t + 1) * NODES)
+                if v == 1:
+                    pair = work.tile([ENCODED, NODES], F32, name="pair")
+                    nc.vector.tensor_add(pair[:], encoded[:, before], encoded[:, block])
+                if v == 2:
+                    nc.vector.tensor_add(summed[:, step], pair[:], encoded[:, block])
+                    store_queue = nc.scalar if t == 0 else nc.sync
+                    store_queue.dma_start(out[:, step], summed[:, step])

@@ -9,9 +9,8 @@ FEATURES = 128
 ENCODED = 128
 STEPS, VEHICLES, NODES = 2, 3, 128
 PICKED = STEPS * VEHICLES * NODES
-BLOCKS = STEPS * VEHICLES
 BLOCK_COLUMNS = NODES // 16
-PIECE_BLOCKS = (3, 2, 1)
+PIECE_BLOCKS = (2, 2, 2)
 SLOPE = 0.01
 
 FLOPS = 2 * FEATURES * ENCODED * PICKED

@@ -10,7 +10,8 @@ ENCODED = 128
 STEPS, VEHICLES, NODES = 2, 3, 128
 PICKED = STEPS * VEHICLES * NODES
 BLOCK_COLUMNS = NODES // 16
-PIECE_BLOCKS = (2, 2, 2)
+PIECE_BLOCKS = 2
+PIECE_STARTS = (0, 4, 2)
 SLOPE = 0.01
 
 FLOPS = 2 * FEATURES * ENCODED * PICKED
@@ -39,32 +40,33 @@ def tile_gnnbase_kernel(tc, table, wn, bn, offs, out):
         biased = held.tile([ENCODED, PICKED], F32, name="biased")
         encoded = held.tile([ENCODED, PICKED], F32, name="encoded")
         summed = held.tile([ENCODED, STEPS * NODES], F32, name="summed")
-        first = 0
-        for blocks in PIECE_BLOCKS:
-            projected = psum.tile([ENCODED, max(PIECE_BLOCKS) * NODES], F32, name="projected")
-            piece = offsets[:, first * BLOCK_COLUMNS : (first + blocks) * BLOCK_COLUMNS]
-            nc.tensor.matmul(
-                projected[:, 0 : blocks * NODES], weights[:], store[:].indirect(piece), start=True, stop=True
-            )
+        running = [None] * STEPS
+        added = [0] * STEPS
+        for first in PIECE_STARTS:
+            projected = psum.tile([ENCODED, PIECE_BLOCKS * NODES], F32, name="projected")
+            piece = offsets[:, first * BLOCK_COLUMNS : (first + PIECE_BLOCKS) * BLOCK_COLUMNS]
+            nc.tensor.matmul(projected[:], weights[:], store[:].indirect(piece), start=True, stop=True)
 
-            for b in range(first, first + blocks):
+            for b in range(first, first + PIECE_BLOCKS):
                 block = slice(b * NODES, (b + 1) * NODES)
                 in_piece = slice((b - first) * NODES, (b - first + 1) * NODES)
                 nc.scalar.activation(biased[:, block], projected[:, in_piece], IDENTITY, bias=bias[:])
                 nc.vector.scalar_tensor_tensor(
                     encoded[:, block], biased[:, block], SLOPE, biased[:, block], ALU.mult, ALU.max
                 )
-            first += blocks
 
-            for b in range(first - blocks, first):
-                t, v = divmod(b, VEHICLES)
+            for b in range(first, first + PIECE_BLOCKS):
+                t = b // VEHICLES
                 block = slice(b * NODES, (b + 1) * NODES)
-                before = slice((b - 1) * NODES, b * NODES)
                 step = slice(t * NODES, (t + 1) * NODES)
-                if v == 1:
+                added[t] += 1
+                if added[t] == 1:
+                    running[t] = encoded[:, block]
+                elif added[t] < VEHICLES:
                     pair = work.tile([ENCODED, NODES], F32, name="pair")
-                    nc.vector.tensor_add(pair[:], encoded[:, before], encoded[:, block])
-                if v == 2:
-                    nc.vector.tensor_add(summed[:, step], pair[:], encoded[:, block])
+                    nc.vector.tensor_add(pair[:], running[t], encoded[:, block])
+                    running[t] = pair[:]
+                else:
+                    nc.vector.tensor_add(summed[:, step], running[t], encoded[:, block])
                     store_queue = nc.scalar if t == 0 else nc.sync
                     store_queue.dma_start(out[:, step], summed[:, step])

@@ -25,13 +25,13 @@ def tile_gnnbase_kernel(tc, table, wn, bn, offs, out):
         tc.psum_pool(name="psum", bufs=3) as psum,
     ):
         store = held.tile([FEATURES, STORED], BF16, name="store")
-        nc.scalar.dma_start(store[:], table)
+        nc.sync.dma_start(store[:], table)
         offsets = held.tile([128, PICKED // 16], U16, name="offsets")
         nc.sync.dma_start(offsets[:], offs)
         weights = held.tile([FEATURES, ENCODED], BF16, name="weights")
-        nc.sync.dma_start(weights[:], wn)
+        nc.scalar.dma_start(weights[:], wn)
         bias = held.tile([ENCODED, 1], F32, name="bias")
-        nc.sync.dma_start(bias[:], bn)
+        nc.scalar.dma_start(bias[:], bn)
 
         scratch = held.tile([ENCODED, 1], F32, name="scratch")
         nc.vector.memset(scratch[:], 0.0)

@@ -29,7 +29,7 @@ def tile_gnnbase_kernel(tc, table, wn, bn, offs, out):
         offsets = held.tile([128, PICKED // 16], U16, name="offsets")
         nc.sync.dma_start(offsets[:], offs)
         weights = held.tile([FEATURES, ENCODED], BF16, name="weights")
-        nc.scalar.dma_start(weights[:], wn)
+        nc.sync.dma_start(weights[:], wn)
         bias = held.tile([ENCODED, 1], F32, name="bias")
         nc.scalar.dma_start(bias[:], bn)
 

@@ -28,10 +28,10 @@ def tile_gnnbase_kernel(tc, table, wn, bn, offs, out):
         nc.sync.dma_start(store[:], table)
         offsets = held.tile([128, PICKED // 16], U16, name="offsets")
         nc.sync.dma_start(offsets[:], offs)
-        weights = held.tile([FEATURES, ENCODED], BF16, name="weights")
-        nc.sync.dma_start(weights[:], wn)
         bias = held.tile([ENCODED, 1], F32, name="bias")
-        nc.scalar.dma_start(bias[:], bn)
+        nc.sync.dma_start(bias[:], bn)
+        weights = held.tile([FEATURES, ENCODED], BF16, name="weights")
+        nc.scalar.dma_start(weights[:], wn)
 
         scratch = held.tile([ENCODED, 1], F32, name="scratch")
         nc.vector.memset(scratch[:], 0.0)

import concourse.mybir as mybir

BF16, F32, U16 = mybir.dt.bfloat16, mybir.dt.float32, mybir.dt.uint16
ALU = mybir.AluOpType
IDENTITY = mybir.ActivationFunctionType.Identity

STORED = 2048
FEATURES = 128
ENCODED = 128
STEPS, VEHICLES, NODES = 2, 3, 128
PICKED = STEPS * VEHICLES * NODES
BLOCK_COLUMNS = NODES // 16
PIECE_BLOCKS = 2
PIECE_STARTS = (0, 4, 2)
SLOPE = 0.01

FLOPS = 2 * FEATURES * ENCODED * PICKED


def tile_gnnbase_kernel(tc, table, wn, bn, offs, out):
    nc = tc.nc
    with (
        tc.tile_pool(name="held", bufs=1) as held,
        tc.tile_pool(name="work", bufs=2) as work,
        tc.psum_pool(name="psum", bufs=3) as psum,
    ):
        store = held.tile([FEATURES, STORED], BF16, name="store")
        nc.sync.dma_start(store[:], table)
        offsets = held.tile([128, PICKED // 16], U16, name="offsets")
        nc.sync.dma_start(offsets[:], offs)
        bias = held.tile([ENCODED, 1], F32, name="bias")
        nc.sync.dma_start(bias[:], bn)
        weights = held.tile([FEATURES, ENCODED], BF16, name="weights")
        nc.scalar.dma_start(weights[:], wn)

        scratch = held.tile([ENCODED, 1], F32, name="scratch")
        nc.vector.memset(scratch[:], 0.0)
        nc.scalar.activation(scratch[:], scratch[:], IDENTITY)

        biased = held.tile([ENCODED, PICKED], F32, name="biased")
        encoded = held.tile([ENCODED, PICKED], F32, name="encoded")
        summed = held.tile([ENCODED, STEPS * NODES], F32, name="summed")
        running = [None] * STEPS
        added = [0] * STEPS
        for first in PIECE_STARTS:
            projected = psum.tile([ENCODED, PIECE_BLOCKS * NODES], F32, name="projected")
            piece = offsets[:, first * BLOCK_COLUMNS : (first + PIECE_BLOCKS) * BLOCK_COLUMNS]
            nc.tensor.matmul(projected[:], weights[:], store[:].indirect(piece), start=True, stop=True)

            for b in range(first, first + PIECE_BLOCKS):
                block = slice(b * NODES, (b + 1) * NODES)
                in_piece = slice((b - first) * NODES, (b - first + 1) * NODES)
                nc.scalar.activation(biased[:, block], projected[:, in_piece], IDENTITY, bias=bias[:])
                nc.vector.scalar_tensor_tensor(
                    encoded[:, block], biased[:, block], SLOPE, biased[:, block], ALU.mult, ALU.max
                )

            for b in range(first, first + PIECE_BLOCKS):
                t = b // VEHICLES
                block = slice(b * NODES, (b + 1) * NODES)
                step = slice(t * NODES, (t + 1) * NODES)
                added[t] += 1
                if added[t] == 1:
                    running[t] = encoded[:, block]
                elif added[t] < VEHICLES:
                    pair = work.tile([ENCODED, NODES], F32, name="pair")
                    nc.vector.tensor_add(pair[:], running[t], encoded[:, block])
                    running[t] = pair[:]
                else:
                    nc.vector.tensor_add(summed[:, step], running[t], encoded[:, block])
                    store_queue = nc.scalar if t == 0 else nc.sync
                    store_queue.dma_start(out[:, step], summed[:, step])
